import numpy as np
import ml_dtypes


def mxq(x, axis, fmt="e4m3"):
    dtype, down = {"e4m3": (ml_dtypes.float8_e4m3fn, 7), "e5m2": (ml_dtypes.float8_e5m2, 14)}[fmt]
    v = np.moveaxis(np.asarray(x, np.float32).astype(ml_dtypes.bfloat16).astype(np.float64), axis, -1)
    blocks = v.reshape(v.shape[:-1] + (-1, 32))
    amax = np.abs(blocks).max(-1, keepdims=True)
    byte = np.maximum(np.where(amax > 0, np.frexp(amax)[1] - 1 + 127, 0) - down, 1)
    scale = np.exp2(byte - 127.0)
    codes = (blocks / scale).astype(np.float32).astype(dtype).astype(np.float64)
    return np.moveaxis((codes * scale).reshape(v.shape), -1, axis)


WIDE = False


def mx_kscale(k):
    if not WIDE:
        return np.ones(k)
    levels = np.array([10, -10, 5, -5, 0])
    a = np.random.permutation(np.resize(levels, k // 512 * 4)).reshape(k // 512, 4)
    idx = np.arange(k)
    return np.exp2(a[idx // 512, idx % 128 // 32])


BF16 = ml_dtypes.bfloat16


def bf(x):
    return np.asarray(x, np.float32).astype(BF16)


def f64(x):
    return np.asarray(x).astype(np.float64)


E2M1 = np.array([0.0, 0.5, 1.0, 1.5, 2.0, 3.0, 4.0, 6.0, -0.0, -0.5, -1.0, -1.5, -2.0, -3.0, -4.0, -6.0])


def pack_weight(w, fmt):
    k, n = w.shape
    w = f64(bf(w)).reshape(k // 32, 32, n)
    amax = np.abs(w).max(1)
    if fmt == "e4m3":
        byte = np.frexp(amax)[1] - 1 + 127 - 7
    else:
        mant, ex = np.frexp(amax / 6.0)
        byte = np.where(mant > 0.5, ex, ex - 1) + 127
    byte = np.clip(np.where(amax > 0, byte, 1), 1, 254)
    scaled = (w * np.exp2(127.0 - byte)[:, None, :]).reshape(k, n).astype(np.float32)
    by_word = np.ascontiguousarray(scaled.reshape(k // 512, 128, 4, n).transpose(0, 1, 3, 2))
    if fmt == "e4m3":
        words = by_word.astype(ml_dtypes.float8_e4m3fn).view(np.uint8)
    else:
        c = by_word.astype(ml_dtypes.float4_e2m1fn).view(np.uint8) & 0xF
        words = c[..., 0::2] | (c[..., 1::2] << 4)
    return np.ascontiguousarray(words), np.ascontiguousarray(byte.astype(np.uint8).reshape(k // 512, 16, n))


def unpack_weight(words, scales, fmt):
    g, p, n, _ = words.shape
    if fmt == "e4m3":
        vals = np.ascontiguousarray(words).view(ml_dtypes.float8_e4m3fn).astype(np.float64)
    else:
        nib = np.empty((g, p, n, 4), np.uint8)
        nib[..., 0::2] = words & 0xF
        nib[..., 1::2] = words >> 4
        vals = E2M1[nib]
    vals = vals * np.repeat(np.exp2(scales.astype(np.float64) - 127.0), 8, axis=1)[..., None]
    return vals.transpose(0, 1, 3, 2).reshape(g * 512, n)


B, T, C, CO, HS, DW, DA, DV, DG = 4, 128, 2048, 2048, 64, 128, 128, 128, 256
H = C // HS
EPS_GN = 0.00064


def setup_inputs():
    n = np.random.standard_normal
    t = mx_kscale(C)
    inputs = {
        "y": bf(n((B, T, C)) * 0.1),
        "r": bf(n((B, T, C))),
        "k": bf(n((B, T, C)) * 0.6),
        "v": bf(n((B, T, C)) * 0.8),
        "g_hid": bf(1.0 / (1.0 + np.exp(-n((B, T, DG))))),
        "g2": bf(n((DG, C)) * 2.0 / np.sqrt(DG) * t),
        "r_k": bf(n((H, HS)) * 0.2 - 0.04),
        "ln_g": bf(1.0 + n((C,)) * 0.1),
        "ln_b": bf(n((C,)) * 0.1),
    }
    w_o = n((CO, C)) * 0.7 / np.sqrt(C) / t
    words, scales = pack_weight(np.ascontiguousarray(w_o.T), "e4m3")
    inputs["W_o_words"] = words
    inputs["W_o_scales"] = scales
    return inputs


def reference(y, r, k, v, g_hid, g2, r_k, ln_g, ln_b, W_o_words, W_o_scales):
    yh = f64(y).reshape(B, T, H, HS)
    mu = np.mean(yh, axis=-1, keepdims=True)
    var = np.mean((yh - mu) ** 2, axis=-1, keepdims=True)
    yn = ((yh - mu) / np.sqrt(var + EPS_GN)).reshape(B, T, C)
    yn = yn * f64(ln_g) + f64(ln_b)
    rh = f64(r).reshape(B, T, H, HS)
    kh = f64(k).reshape(B, T, H, HS)
    vh = f64(v).reshape(B, T, H, HS)
    dot = np.sum(rh * kh * f64(r_k), axis=-1, keepdims=True)
    y2 = yn + (dot * vh).reshape(B, T, C)
    g = f64(g_hid) @ f64(g2)
    z = y2 * g
    return mxq(z, 2, "e4m3") @ unpack_weight(W_o_words, W_o_scales, "e4m3")

@@ -1,0 +1,248 @@
+from contextlib import ExitStack
+
+import concourse.mybir as mybir
+from concourse.masks import make_identity
+
+F32 = mybir.dt.float32
+BF16 = mybir.dt.bfloat16
+I32 = mybir.dt.int32
+U32 = mybir.dt.uint32
+U8 = mybir.dt.uint8
+FP8X4 = mybir.dt.float8_e4m3fn_x4
+ACT = mybir.ActivationFunctionType
+ALU = mybir.AluOpType
+AXIS = mybir.AxisListType
+
+P = 128
+PACK = 4
+K_PASS = P * PACK
+TILES = 4
+CH = 2048
+GROUPS = CH // K_PASS
+HEAD = 64
+HEADS = CH // HEAD
+HEADS_PER_GROUP = K_PASS // HEAD
+ROWS_PER_HEAD = HEAD // PACK
+HID = 256
+HID_HALVES = HID // P
+N_TILE = 512
+N_TILES = CH // N_TILE
+EPS_GN = 0.00064
+
+FLOPS = 2 * TILES * P * CH * CH + 2 * TILES * P * HID * CH
+
+
+def tile_full_tmix_params_pc_kernel(
+    tc, y, r, k, v, g_hid, g2, r_k, ln_g, ln_b, W_o_words, W_o_scales, out
+):
+    nc = tc.nc
+    with ExitStack() as stack:
+        const = stack.enter_context(tc.tile_pool(name="const", bufs=1))
+        inputs = stack.enter_context(tc.tile_pool(name="inputs", bufs=TILES))
+        small = stack.enter_context(tc.tile_pool(name="small", bufs=2))
+        token = stack.enter_context(tc.tile_pool(name="token", bufs=2))
+        chan = stack.enter_context(tc.tile_pool(name="chan", bufs=3))
+        quant = stack.enter_context(tc.tile_pool(name="quant", bufs=2))
+        result = stack.enter_context(tc.tile_pool(name="result", bufs=4))
+        unit_psum = stack.enter_context(tc.psum_pool(name="unit_psum", bufs=2))
+        acc_psum = stack.enter_context(tc.psum_pool(name="acc_psum", bufs=2))
+
+        y_sb, r_sb, k_sb, v_sb = [], [], [], []
+
+        def load_token_tile(i):
+            for name, src, dst in (("r", r, r_sb), ("k", k, k_sb), ("y", y, y_sb), ("v", v, v_sb)):
+                t_in = inputs.tile([P, CH], BF16, name="%s_sb" % name, tag=name)
+                nc.sync.dma_start(out=t_in[:], in_=src[i])
+                dst.append(t_in)
+
+        w_codes = const.tile([P, GROUPS, CH], U32, align_bytes=64)
+        w_words = W_o_words.rearrange("g p n t -> p g (n t)")
+
+        def load_w_columns(nt):
+            nc.sync.dma_start(
+                out=w_codes[:, :, nt * N_TILE : (nt + 1) * N_TILE].bitcast(I32),
+                in_=w_words[:, :, nt * N_TILE * PACK : (nt + 1) * N_TILE * PACK].bitcast(I32),
+            )
+
+        w_planes = const.tile([P, CH], U8, align_bytes=64)
+        nc.vector.memset(w_planes[:].bitcast(I32), 0)
+        ln_rows = const.tile([P, K_PASS], BF16)
+        nc.vector.memset(ln_rows[:], 0.0)
+
+        load_token_tile(0)
+        rk_bc = const.tile([P, CH], BF16)
+        nc.sync.dma_start(out=rk_bc[:], in_=r_k.rearrange("h c -> (h c)").partition_broadcast(P))
+        nc.sync.dma_start(out=ln_rows[0:GROUPS, :], in_=ln_g.rearrange("(g c) -> g c", g=GROUPS))
+        nc.sync.dma_start(
+            out=ln_rows[GROUPS : 2 * GROUPS, :], in_=ln_b.rearrange("(g c) -> g c", g=GROUPS)
+        )
+        gh_raw = const.tile([P, TILES, HID], BF16)
+        nc.sync.dma_start(out=gh_raw[:], in_=g_hid.rearrange("b t j -> t b j"))
+        g2_raw = const.tile([P, HID_HALVES, CH], BF16)
+        for jh in range(HID_HALVES):
+            nc.sync.dma_start(out=g2_raw[:, jh, :], in_=g2[jh * P : (jh + 1) * P, :])
+        load_token_tile(1)
+        for q in range(4):
+            nc.sync.dma_start(
+                out=w_planes[32 * q : 32 * q + 16, :].bitcast(I32),
+                in_=W_o_scales[:, 4 * q : 4 * q + 4, :].bitcast(I32),
+            )
+        load_w_columns(0)
+        load_w_columns(1)
+        load_token_tile(2)
+        load_w_columns(2)
+        load_w_columns(3)
+        load_token_tile(3)
+
+        ident_f32 = const.tile([P, P], F32)
+        make_identity(nc, ident_f32[:])
+        ident_bf = const.tile([P, P], BF16)
+        make_identity(nc, ident_bf[:])
+
+        ln_sorted = const.tile([P, PACK, P], F32)
+        nc.vector.tensor_copy(out=ln_sorted[:], in_=ln_rows[:].rearrange("p (q t) -> p t q", t=PACK))
+        ln_ps = unit_psum.tile([P, PACK, P], F32, tag="nT")
+        for t in range(PACK):
+            nc.tensor.transpose(ln_ps[:, t, :], ln_sorted[:, t, :], ident_f32[:])
+        chan_affine = const.tile([P, PACK, 2 * GROUPS], F32)
+        nc.vector.tensor_copy(out=chan_affine[:], in_=ln_ps[:, :, 0 : 2 * GROUPS])
+
+        gh_ps = unit_psum.tile([P, HID_HALVES, TILES * P], BF16, tag="wT")
+        for i in range(TILES):
+            for jh in range(HID_HALVES):
+                nc.tensor.transpose(
+                    gh_ps[:, jh, i * P : (i + 1) * P], gh_raw[:, i, jh * P : (jh + 1) * P], ident_bf[:]
+                )
+        ghT = const.tile([P, HID_HALVES, TILES * P], BF16)
+        nc.vector.tensor_copy(out=ghT[:], in_=gh_ps[:])
+
+        g2_sorted = const.tile([P, HID_HALVES, GROUPS, PACK, P], BF16)
+        for jh in range(HID_HALVES):
+            nc.scalar.copy(
+                out=g2_sorted[:, jh],
+                in_=g2_raw[:, jh, :].rearrange("p (g q t) -> p g t q", g=GROUPS, t=PACK),
+            )
+
+        for i in range(TILES):
+            stats = small.tile([P, HEADS, 6], F32)
+            for h in range(HEADS):
+                nc.vector.bn_stats(out=stats[:, h, :], in_=y_sb[i][:, h * HEAD : (h + 1) * HEAD])
+            mean_even, m2_even = stats[:, :, 1], stats[:, :, 2]
+            mean_odd, m2_odd = stats[:, :, 4], stats[:, :, 5]
+            diff = small.tile([P, HEADS], F32)
+            nc.vector.tensor_sub(out=diff[:], in0=mean_even, in1=mean_odd)
+            m2 = small.tile([P, HEADS], F32)
+            nc.vector.scalar_tensor_tensor(
+                out=m2[:], in0=m2_even, scalar=HEAD * EPS_GN, in1=m2_odd, op0=ALU.add, op1=ALU.add
+            )
+            nc.vector.tensor_mul(out=diff[:], in0=diff[:], in1=diff[:])
+            nc.vector.scalar_tensor_tensor(
+                out=m2[:], in0=diff[:], scalar=HEAD / 4.0, in1=m2[:], op0=ALU.mult, op1=ALU.add
+            )
+            std = small.tile([P, HEADS], F32)
+            nc.scalar.activation(out=std[:], in_=m2[:], func=ACT.Sqrt, scale=1.0 / HEAD)
+            rstd = small.tile([P, HEADS], F32)
+            nc.vector.reciprocal(out=rstd[:], in_=std[:])
+            mean2 = small.tile([P, HEADS], F32)
+            nc.vector.tensor_add(out=mean2[:], in0=mean_even, in1=mean_odd)
+            shift = small.tile([P, HEADS], F32)
+            nc.vector.scalar_tensor_tensor(
+                out=shift[:], in0=mean2[:], scalar=-0.5, in1=rstd[:], op0=ALU.mult, op1=ALU.mult
+            )
+
+            prod = token.tile([P, CH], F32)
+            dot = small.tile([P, HEADS], F32)
+            for g in range(GROUPS):
+                cols = slice(g * K_PASS, (g + 1) * K_PASS)
+                nc.gpsimd.tensor_tensor(out=prod[:, cols], in0=r_sb[i][:, cols], in1=k_sb[i][:, cols], op=ALU.mult)
+                second = nc.gpsimd if g % 2 == 0 else nc.vector
+                second.tensor_tensor(out=prod[:, cols], in0=prod[:, cols], in1=rk_bc[:, cols], op=ALU.mult)
+                nc.vector.tensor_reduce(
+                    out=dot[:, g * HEADS_PER_GROUP : (g + 1) * HEADS_PER_GROUP],
+                    in_=prod[:, cols].rearrange("p (h c) -> p h c", c=HEAD),
+                    axis=AXIS.X,
+                    op=ALU.add,
+                )
+
+            norm = token.tile([P, GROUPS, PACK, P], F32)
+            bonus = token.tile([P, GROUPS, PACK, P], F32)
+            for h in range(HEADS):
+                g, hh = divmod(h, HEADS_PER_GROUP)
+                rows = slice(hh * ROWS_PER_HEAD, (hh + 1) * ROWS_PER_HEAD)
+                head_cols = slice(h * HEAD, (h + 1) * HEAD)
+                nc.scalar.activation(
+                    out=norm[:, g, :, rows],
+                    in_=y_sb[i][:, head_cols].rearrange("p (q t) -> p t q", t=PACK),
+                    func=ACT.Identity,
+                    scale=rstd[:, h : h + 1],
+                    bias=shift[:, h : h + 1],
+                )
+            for h in range(HEADS):
+                g, hh = divmod(h, HEADS_PER_GROUP)
+                rows = slice(hh * ROWS_PER_HEAD, (hh + 1) * ROWS_PER_HEAD)
+                head_cols = slice(h * HEAD, (h + 1) * HEAD)
+                nc.scalar.activation(
+                    out=bonus[:, g, :, rows],
+                    in_=v_sb[i][:, head_cols].rearrange("p (q t) -> p t q", t=PACK),
+                    func=ACT.Copy,
+                    scale=dot[:, h : h + 1],
+                )
+
+            z_codes = quant.tile([P, GROUPS, P], U32, align_bytes=64)
+            z_scales = quant.tile([P, GROUPS, P], U8, align_bytes=64)
+            for g in range(GROUPS):
+                normT = unit_psum.tile([P, PACK, P], F32, tag="nT")
+                for t in range(PACK):
+                    nc.tensor.transpose(normT[:, t, :], norm[:, g, t, :], ident_f32[:])
+                bonusT = unit_psum.tile([P, PACK, P], F32, tag="wT")
+                for t in range(PACK):
+                    nc.tensor.transpose(bonusT[:, t, :], bonus[:, g, t, :], ident_f32[:])
+                gateT = unit_psum.tile([P, PACK, P], F32, tag="gT")
+                for t in range(PACK):
+                    for jh in range(HID_HALVES):
+                        nc.tensor.matmul(
+                            gateT[:, t, :],
+                            lhsT=g2_sorted[:, jh, g, t, :],
+                            rhs=ghT[:, jh, i * P : (i + 1) * P],
+                            start=(jh == 0),
+                            stop=(jh == HID_HALVES - 1),
+                        )
+                y2T = chan.tile([P, PACK, P], F32)
+                for t in range(PACK):
+                    nc.scalar.activation(
+                        out=y2T[:, t, :],
+                        in_=normT[:, t, :],
+                        func=ACT.Identity,
+                        scale=chan_affine[:, t, g : g + 1],
+                        bias=chan_affine[:, t, GROUPS + g : GROUPS + g + 1],
+                    )
+                nc.vector.tensor_tensor(out=y2T[:], in0=y2T[:], in1=bonusT[:], op=ALU.add)
+                zT = chan.tile([P, P, PACK], BF16, align_bytes=64)
+                nc.vector.tensor_tensor(
+                    out=zT[:],
+                    in0=y2T[:].rearrange("p t m -> p m t"),
+                    in1=gateT[:].rearrange("p t m -> p m t"),
+                    op=ALU.mult,
+                )
+                nc.vector.quantize_mx(
+                    out=z_codes[:, g, :].bitcast(FP8X4),
+                    scales=z_scales[:, g, :],
+                    in_=zT[:].rearrange("p m t -> p (m t)"),
+                )
+
+            for nt in range(N_TILES):
+                n_cols = slice(nt * N_TILE, (nt + 1) * N_TILE)
+                acc = acc_psum.tile([P, N_TILE], F32)
+                for g in range(GROUPS):
+                    nc.tensor.matmul_mx(
+                        out=acc[:],
+                        lhsT=z_codes[:, g, :].bitcast(FP8X4),
+                        lhsT_scale=z_scales[:, g, :],
+                        rhs=w_codes[:, g, n_cols].bitcast(FP8X4),
+                        rhs_scale=w_planes[PACK * g : P, n_cols],
+                        start=(g == 0),
+                        stop=(g == GROUPS - 1),
+                    )
+                out_sb = result.tile([P, N_TILE], F32)
+                nc.scalar.copy(out=out_sb[:], in_=acc[:])
+                nc.sync.dma_start(out=out[i][:, n_cols], in_=out_sb[:])

@@ -27,6 +27,7 @@ HID = 256
 HID_HALVES = HID // P
 N_TILE = 512
 N_TILES = CH // N_TILE
+UNITS = TILES * GROUPS
 EPS_GN = 0.00064
 
 FLOPS = 2 * TILES * P * CH * CH + 2 * TILES * P * HID * CH
@@ -37,23 +38,39 @@ def tile_full_tmix_params_pc_kernel(
 ):
     nc = tc.nc
     with ExitStack() as stack:
+        stack.enter_context(tc.manual_schedule())
         const = stack.enter_context(tc.tile_pool(name="const", bufs=1))
         inputs = stack.enter_context(tc.tile_pool(name="inputs", bufs=TILES))
         small = stack.enter_context(tc.tile_pool(name="small", bufs=2))
-        token = stack.enter_context(tc.tile_pool(name="token", bufs=2))
-        chan = stack.enter_context(tc.tile_pool(name="chan", bufs=3))
+        token = stack.enter_context(tc.tile_pool(name="token", bufs=3))
+        chan = stack.enter_context(tc.tile_pool(name="chan", bufs=2))
         quant = stack.enter_context(tc.tile_pool(name="quant", bufs=2))
-        result = stack.enter_context(tc.tile_pool(name="result", bufs=4))
+        result = stack.enter_context(tc.tile_pool(name="result", bufs=3))
         unit_psum = stack.enter_context(tc.psum_pool(name="unit_psum", bufs=2))
         acc_psum = stack.enter_context(tc.psum_pool(name="acc_psum", bufs=2))
 
-        y_sb, r_sb, k_sb, v_sb = [], [], [], []
+        w_planes = const.tile([P, CH], U8, align_bytes=64)
+        nc.vector.memset(w_planes[:].bitcast(I32), 0)
+        rk_row = const.tile([P, CH], BF16)
+        nc.vector.memset(rk_row[:], 0.0)
+        ln_rows = const.tile([P, K_PASS], BF16)
+        nc.vector.memset(ln_rows[:], 0.0)
+        ones = const.tile([P, P], BF16)
+        nc.vector.memset(ones[:], 1.0)
+        one_col = const.tile([P, 1], F32)
+        nc.vector.memset(one_col[:], 1.0)
+
+        y_sb, r_sb, k_sb, v_sb = {}, {}, {}, {}
+
+        def load(dst, src, i, name):
+            dst[i] = inputs.tile([P, CH], BF16, name="%s_sb" % name, tag=name)
+            nc.sync.dma_start(out=dst[i][:], in_=src[i])
 
         def load_token_tile(i):
-            for name, src, dst in (("r", r, r_sb), ("k", k, k_sb), ("y", y, y_sb), ("v", v, v_sb)):
-                t_in = inputs.tile([P, CH], BF16, name="%s_sb" % name, tag=name)
-                nc.sync.dma_start(out=t_in[:], in_=src[i])
-                dst.append(t_in)
+            load(y_sb, y, i, "y")
+            load(r_sb, r, i, "r")
+            load(k_sb, k, i, "k")
+            load(v_sb, v, i, "v")
 
         w_codes = const.tile([P, GROUPS, CH], U32, align_bytes=64)
         w_words = W_o_words.rearrange("g p n t -> p g (n t)")
@@ -64,24 +81,19 @@ def tile_full_tmix_params_pc_kernel(
                 in_=w_words[:, :, nt * N_TILE * PACK : (nt + 1) * N_TILE * PACK].bitcast(I32),
             )
 
-        w_planes = const.tile([P, CH], U8, align_bytes=64)
-        nc.vector.memset(w_planes[:].bitcast(I32), 0)
-        ln_rows = const.tile([P, K_PASS], BF16)
-        nc.vector.memset(ln_rows[:], 0.0)
-
-        load_token_tile(0)
-        rk_bc = const.tile([P, CH], BF16)
-        nc.sync.dma_start(out=rk_bc[:], in_=r_k.rearrange("h c -> (h c)").partition_broadcast(P))
+        nc.sync.dma_start(out=rk_row[0:1, :], in_=r_k.rearrange("h c -> (h c)").unsqueeze(0))
         nc.sync.dma_start(out=ln_rows[0:GROUPS, :], in_=ln_g.rearrange("(g c) -> g c", g=GROUPS))
         nc.sync.dma_start(
             out=ln_rows[GROUPS : 2 * GROUPS, :], in_=ln_b.rearrange("(g c) -> g c", g=GROUPS)
         )
         gh_raw = const.tile([P, TILES, HID], BF16)
         nc.sync.dma_start(out=gh_raw[:], in_=g_hid.rearrange("b t j -> t b j"))
+        load_token_tile(0)
         g2_raw = const.tile([P, HID_HALVES, CH], BF16)
         for jh in range(HID_HALVES):
             nc.sync.dma_start(out=g2_raw[:, jh, :], in_=g2[jh * P : (jh + 1) * P, :])
         load_token_tile(1)
+        load_token_tile(2)
         for q in range(4):
             nc.sync.dma_start(
                 out=w_planes[32 * q : 32 * q + 16, :].bitcast(I32),
@@ -89,160 +101,248 @@ def tile_full_tmix_params_pc_kernel(
             )
         load_w_columns(0)
         load_w_columns(1)
-        load_token_tile(2)
+        load(y_sb, y, 3, "y")
         load_w_columns(2)
         load_w_columns(3)
-        load_token_tile(3)
+        load(r_sb, r, 3, "r")
+        load(k_sb, k, 3, "k")
+        load(v_sb, v, 3, "v")
 
         ident_f32 = const.tile([P, P], F32)
         make_identity(nc, ident_f32[:])
         ident_bf = const.tile([P, P], BF16)
         make_identity(nc, ident_bf[:])
 
+        nc.scalar.activation(out=one_col[:], in_=one_col[:], func=ACT.Sqrt)
+
+        rk_bc = const.tile([P, CH], BF16)
+        for nt in range(N_TILES):
+            n_cols = slice(nt * N_TILE, (nt + 1) * N_TILE)
+            rk_ps = acc_psum.tile([P, N_TILE], F32, tag="acc")
+            nc.tensor.matmul(rk_ps[:], lhsT=ones[:], rhs=rk_row[:, n_cols], start=True, stop=True)
+            nc.scalar.copy(out=rk_bc[:, n_cols], in_=rk_ps[:])
+
         ln_sorted = const.tile([P, PACK, P], F32)
         nc.vector.tensor_copy(out=ln_sorted[:], in_=ln_rows[:].rearrange("p (q t) -> p t q", t=PACK))
-        ln_ps = unit_psum.tile([P, PACK, P], F32, tag="nT")
+        ln_ps = unit_psum.tile([P, PACK, P], F32, tag="normT")
         for t in range(PACK):
             nc.tensor.transpose(ln_ps[:, t, :], ln_sorted[:, t, :], ident_f32[:])
         chan_affine = const.tile([P, PACK, 2 * GROUPS], F32)
-        nc.vector.tensor_copy(out=chan_affine[:], in_=ln_ps[:, :, 0 : 2 * GROUPS])
 
-        gh_ps = unit_psum.tile([P, HID_HALVES, TILES * P], BF16, tag="wT")
+        gh_ps = unit_psum.tile([P, HID_HALVES, TILES * P], BF16, tag="bonusT")
         for i in range(TILES):
             for jh in range(HID_HALVES):
                 nc.tensor.transpose(
                     gh_ps[:, jh, i * P : (i + 1) * P], gh_raw[:, i, jh * P : (jh + 1) * P], ident_bf[:]
                 )
         ghT = const.tile([P, HID_HALVES, TILES * P], BF16)
-        nc.vector.tensor_copy(out=ghT[:], in_=gh_ps[:])
-
         g2_sorted = const.tile([P, HID_HALVES, GROUPS, PACK, P], BF16)
-        for jh in range(HID_HALVES):
-            nc.scalar.copy(
-                out=g2_sorted[:, jh],
-                in_=g2_raw[:, jh, :].rearrange("p (g q t) -> p g t q", g=GROUPS, t=PACK),
-            )
 
-        for i in range(TILES):
-            stats = small.tile([P, HEADS, 6], F32)
-            for h in range(HEADS):
-                nc.vector.bn_stats(out=stats[:, h, :], in_=y_sb[i][:, h * HEAD : (h + 1) * HEAD])
-            mean_even, m2_even = stats[:, :, 1], stats[:, :, 2]
-            mean_odd, m2_odd = stats[:, :, 4], stats[:, :, 5]
-            diff = small.tile([P, HEADS], F32)
+        stats, m2, mean2, std, rstd, shift = {}, {}, {}, {}, {}, {}
+        prod, dot, norm, bonus = {}, {}, {}, {}
+        normT, bonusT, gateT, y2T = {}, {}, {}, {}
+        zT, z_codes, z_scales, acc = {}, {}, {}, {}
+
+        def head_stats(u):
+            if not 0 <= u < UNITS:
+                return
+            i, g = divmod(u, GROUPS)
+            if g == 0:
+                stats[i] = small.tile([P, HEADS, 6], F32, name="stats", tag="stats")
+            for h in range(g * HEADS_PER_GROUP, (g + 1) * HEADS_PER_GROUP):
+                nc.vector.bn_stats(out=stats[i][:, h, :], in_=y_sb[i][:, h * HEAD : (h + 1) * HEAD])
+
+        def variance_sums(i):
+            if not 0 <= i < TILES:
+                return
+            mean_even, m2_even = stats[i][:, :, 1], stats[i][:, :, 2]
+            mean_odd, m2_odd = stats[i][:, :, 4], stats[i][:, :, 5]
+            diff = small.tile([P, HEADS], F32, name="diff", tag="diff")
+            m2[i] = small.tile([P, HEADS], F32, name="m2", tag="m2")
+            mean2[i] = small.tile([P, HEADS], F32, name="mean2", tag="mean2")
             nc.vector.tensor_sub(out=diff[:], in0=mean_even, in1=mean_odd)
-            m2 = small.tile([P, HEADS], F32)
             nc.vector.scalar_tensor_tensor(
-                out=m2[:], in0=m2_even, scalar=HEAD * EPS_GN, in1=m2_odd, op0=ALU.add, op1=ALU.add
+                out=m2[i][:], in0=m2_even, scalar=HEAD * EPS_GN, in1=m2_odd, op0=ALU.add, op1=ALU.add
             )
             nc.vector.tensor_mul(out=diff[:], in0=diff[:], in1=diff[:])
             nc.vector.scalar_tensor_tensor(
-                out=m2[:], in0=diff[:], scalar=HEAD / 4.0, in1=m2[:], op0=ALU.mult, op1=ALU.add
+                out=m2[i][:], in0=diff[:], scalar=HEAD / 4.0, in1=m2[i][:], op0=ALU.mult, op1=ALU.add
             )
-            std = small.tile([P, HEADS], F32)
-            nc.scalar.activation(out=std[:], in_=m2[:], func=ACT.Sqrt, scale=1.0 / HEAD)
-            rstd = small.tile([P, HEADS], F32)
-            nc.vector.reciprocal(out=rstd[:], in_=std[:])
-            mean2 = small.tile([P, HEADS], F32)
-            nc.vector.tensor_add(out=mean2[:], in0=mean_even, in1=mean_odd)
-            shift = small.tile([P, HEADS], F32)
+            nc.vector.tensor_add(out=mean2[i][:], in0=mean_even, in1=mean_odd)
+
+        def standard_deviation(i):
+            if not 0 <= i < TILES:
+                return
+            std[i] = small.tile([P, HEADS], F32, name="std", tag="std")
+            nc.scalar.activation(out=std[i][:], in_=m2[i][:], func=ACT.Sqrt, scale=1.0 / HEAD)
+
+        def norm_scalars(i):
+            if not 0 <= i < TILES:
+                return
+            rstd[i] = small.tile([P, HEADS], F32, name="rstd", tag="rstd")
+            shift[i] = small.tile([P, HEADS], F32, name="shift", tag="shift")
+            nc.vector.reciprocal(out=rstd[i][:], in_=std[i][:])
             nc.vector.scalar_tensor_tensor(
-                out=shift[:], in0=mean2[:], scalar=-0.5, in1=rstd[:], op0=ALU.mult, op1=ALU.mult
+                out=shift[i][:], in0=mean2[i][:], scalar=-0.5, in1=rstd[i][:], op0=ALU.mult, op1=ALU.mult
             )
 
-            prod = token.tile([P, CH], F32)
-            dot = small.tile([P, HEADS], F32)
-            for g in range(GROUPS):
-                cols = slice(g * K_PASS, (g + 1) * K_PASS)
-                nc.gpsimd.tensor_tensor(out=prod[:, cols], in0=r_sb[i][:, cols], in1=k_sb[i][:, cols], op=ALU.mult)
-                second = nc.gpsimd if g % 2 == 0 else nc.vector
-                second.tensor_tensor(out=prod[:, cols], in0=prod[:, cols], in1=rk_bc[:, cols], op=ALU.mult)
-                nc.vector.tensor_reduce(
-                    out=dot[:, g * HEADS_PER_GROUP : (g + 1) * HEADS_PER_GROUP],
-                    in_=prod[:, cols].rearrange("p (h c) -> p h c", c=HEAD),
-                    axis=AXIS.X,
-                    op=ALU.add,
-                )
+        def dot_products(u):
+            if not 0 <= u < UNITS:
+                return
+            i, g = divmod(u, GROUPS)
+            cols = slice(g * K_PASS, (g + 1) * K_PASS)
+            prod[u] = token.tile([P, K_PASS], F32, name="prod", tag="prod")
+            nc.gpsimd.tensor_tensor(out=prod[u][:], in0=r_sb[i][:, cols], in1=k_sb[i][:, cols], op=ALU.mult)
+            nc.gpsimd.tensor_tensor(out=prod[u][:], in0=prod[u][:], in1=rk_bc[:, cols], op=ALU.mult)
 
-            norm = token.tile([P, GROUPS, PACK, P], F32)
-            bonus = token.tile([P, GROUPS, PACK, P], F32)
-            for h in range(HEADS):
-                g, hh = divmod(h, HEADS_PER_GROUP)
-                rows = slice(hh * ROWS_PER_HEAD, (hh + 1) * ROWS_PER_HEAD)
-                head_cols = slice(h * HEAD, (h + 1) * HEAD)
+        def dot_sums(u):
+            if not 0 <= u < UNITS:
+                return
+            dot[u] = small.tile([P, HEADS_PER_GROUP], F32, name="dot", tag="dot", bufs=4)
+            nc.vector.tensor_reduce(
+                out=dot[u][:], in_=prod[u][:].rearrange("p (h c) -> p h c", c=HEAD), axis=AXIS.X, op=ALU.add
+            )
+
+        def scale_heads(u):
+            if not 0 <= u < UNITS:
+                return
+            i, g = divmod(u, GROUPS)
+            norm[u] = token.tile([P, PACK, P], F32, name="norm", tag="norm")
+            bonus[u] = token.tile([P, PACK, P], F32, name="bonus", tag="bonus")
+            for hh in range(HEADS_PER_GROUP):
+                h = g * HEADS_PER_GROUP + hh
                 nc.scalar.activation(
-                    out=norm[:, g, :, rows],
-                    in_=y_sb[i][:, head_cols].rearrange("p (q t) -> p t q", t=PACK),
+                    out=norm[u][:, :, hh * ROWS_PER_HEAD : (hh + 1) * ROWS_PER_HEAD],
+                    in_=y_sb[i][:, h * HEAD : (h + 1) * HEAD].rearrange("p (q t) -> p t q", t=PACK),
                     func=ACT.Identity,
-                    scale=rstd[:, h : h + 1],
-                    bias=shift[:, h : h + 1],
+                    scale=rstd[i][:, h : h + 1],
+                    bias=shift[i][:, h : h + 1],
                 )
-            for h in range(HEADS):
-                g, hh = divmod(h, HEADS_PER_GROUP)
-                rows = slice(hh * ROWS_PER_HEAD, (hh + 1) * ROWS_PER_HEAD)
-                head_cols = slice(h * HEAD, (h + 1) * HEAD)
+            for hh in range(HEADS_PER_GROUP):
+                h = g * HEADS_PER_GROUP + hh
                 nc.scalar.activation(
-                    out=bonus[:, g, :, rows],
-                    in_=v_sb[i][:, head_cols].rearrange("p (q t) -> p t q", t=PACK),
+                    out=bonus[u][:, :, hh * ROWS_PER_HEAD : (hh + 1) * ROWS_PER_HEAD],
+                    in_=v_sb[i][:, h * HEAD : (h + 1) * HEAD].rearrange("p (q t) -> p t q", t=PACK),
                     func=ACT.Copy,
-                    scale=dot[:, h : h + 1],
+                    scale=dot[u][:, hh : hh + 1],
                 )
 
-            z_codes = quant.tile([P, GROUPS, P], U32, align_bytes=64)
-            z_scales = quant.tile([P, GROUPS, P], U8, align_bytes=64)
+        def sort_gate_columns(g):
+            if not 0 <= g < GROUPS:
+                return
+            for jh in range(HID_HALVES):
+                nc.scalar.copy(
+                    out=g2_sorted[:, jh, g],
+                    in_=g2_raw[:, jh, g * K_PASS : (g + 1) * K_PASS].rearrange("p (q t) -> p t q", t=PACK),
+                )
+
+        def to_channels(u):
+            if not 0 <= u < UNITS:
+                return
+            i, g = divmod(u, GROUPS)
+            normT[u] = unit_psum.tile([P, PACK, P], F32, name="normT", tag="normT")
+            for t in range(PACK):
+                nc.tensor.transpose(normT[u][:, t, :], norm[u][:, t, :], ident_f32[:])
+            bonusT[u] = unit_psum.tile([P, PACK, P], F32, name="bonusT", tag="bonusT")
+            for t in range(PACK):
+                nc.tensor.transpose(bonusT[u][:, t, :], bonus[u][:, t, :], ident_f32[:])
+            gateT[u] = unit_psum.tile([P, PACK, P], F32, name="gateT", tag="gateT")
+            for t in range(PACK):
+                for jh in range(HID_HALVES):
+                    nc.tensor.matmul(
+                        gateT[u][:, t, :],
+                        lhsT=g2_sorted[:, jh, g, t, :],
+                        rhs=ghT[:, jh, i * P : (i + 1) * P],
+                        start=(jh == 0),
+                        stop=(jh == HID_HALVES - 1),
+                    )
+
+        def ln_affine(u):
+            if not 0 <= u < UNITS:
+                return
+            g = u % GROUPS
+            y2T[u] = chan.tile([P, PACK, P], F32, name="y2T", tag="y2T")
+            for t in range(PACK):
+                nc.scalar.activation(
+                    out=y2T[u][:, t, :],
+                    in_=normT[u][:, t, :],
+                    func=ACT.Identity,
+                    scale=chan_affine[:, t, g : g + 1],
+                    bias=chan_affine[:, t, GROUPS + g : GROUPS + g + 1],
+                )
+
+        def gate_and_round(u):
+            if not 0 <= u < UNITS:
+                return
+            i, g = divmod(u, GROUPS)
+            if g == 0:
+                zT[i] = quant.tile([P, GROUPS, P, PACK], BF16, name="zT", tag="zT", align_bytes=64)
+            nc.vector.tensor_tensor(out=y2T[u][:], in0=y2T[u][:], in1=bonusT[u][:], op=ALU.add)
+            nc.vector.tensor_tensor(
+                out=zT[i][:, g],
+                in0=y2T[u][:].rearrange("p t m -> p m t"),
+                in1=gateT[u][:].rearrange("p t m -> p m t"),
+                op=ALU.mult,
+            )
+
+        def quantise(i):
+            if not 0 <= i < TILES:
+                return
+            z_codes[i] = quant.tile([P, GROUPS, P], U32, name="z_codes", tag="z_codes", align_bytes=64)
+            z_scales[i] = quant.tile([P, GROUPS, P], U8, name="z_scales", tag="z_scales", align_bytes=64)
+            nc.vector.quantize_mx(
+                out=z_codes[i][:].rearrange("p g m -> p (g m)").bitcast(FP8X4),
+                scales=z_scales[i][:].rearrange("p g m -> p (g m)"),
+                in_=zT[i][:].rearrange("p g m t -> p (g m t)"),
+            )
+
+        def project(c):
+            if not 0 <= c < TILES * N_TILES:
+                return
+            i, nt = divmod(c, N_TILES)
+            n_cols = slice(nt * N_TILE, (nt + 1) * N_TILE)
+            acc[c] = acc_psum.tile([P, N_TILE], F32, name="acc", tag="acc")
             for g in range(GROUPS):
-                normT = unit_psum.tile([P, PACK, P], F32, tag="nT")
-                for t in range(PACK):
-                    nc.tensor.transpose(normT[:, t, :], norm[:, g, t, :], ident_f32[:])
-                bonusT = unit_psum.tile([P, PACK, P], F32, tag="wT")
-                for t in range(PACK):
-                    nc.tensor.transpose(bonusT[:, t, :], bonus[:, g, t, :], ident_f32[:])
-                gateT = unit_psum.tile([P, PACK, P], F32, tag="gT")
-                for t in range(PACK):
-                    for jh in range(HID_HALVES):
-                        nc.tensor.matmul(
-                            gateT[:, t, :],
-                            lhsT=g2_sorted[:, jh, g, t, :],
-                            rhs=ghT[:, jh, i * P : (i + 1) * P],
-                            start=(jh == 0),
-                            stop=(jh == HID_HALVES - 1),
-                        )
-                y2T = chan.tile([P, PACK, P], F32)
-                for t in range(PACK):
-                    nc.scalar.activation(
-                        out=y2T[:, t, :],
-                        in_=normT[:, t, :],
-                        func=ACT.Identity,
-                        scale=chan_affine[:, t, g : g + 1],
-                        bias=chan_affine[:, t, GROUPS + g : GROUPS + g + 1],
-                    )
-                nc.vector.tensor_tensor(out=y2T[:], in0=y2T[:], in1=bonusT[:], op=ALU.add)
-                zT = chan.tile([P, P, PACK], BF16, align_bytes=64)
-                nc.vector.tensor_tensor(
-                    out=zT[:],
-                    in0=y2T[:].rearrange("p t m -> p m t"),
-                    in1=gateT[:].rearrange("p t m -> p m t"),
-                    op=ALU.mult,
-                )
-                nc.vector.quantize_mx(
-                    out=z_codes[:, g, :].bitcast(FP8X4),
-                    scales=z_scales[:, g, :],
-                    in_=zT[:].rearrange("p m t -> p (m t)"),
+                nc.tensor.matmul_mx(
+                    out=acc[c][:],
+                    lhsT=z_codes[i][:, g, :].bitcast(FP8X4),
+                    lhsT_scale=z_scales[i][:, g, :],
+                    rhs=w_codes[:, g, n_cols].bitcast(FP8X4),
+                    rhs_scale=w_planes[PACK * g : P, n_cols],
+                    start=(g == 0),
+                    stop=(g == GROUPS - 1),
                 )
 
-            for nt in range(N_TILES):
-                n_cols = slice(nt * N_TILE, (nt + 1) * N_TILE)
-                acc = acc_psum.tile([P, N_TILE], F32)
-                for g in range(GROUPS):
-                    nc.tensor.matmul_mx(
-                        out=acc[:],
-                        lhsT=z_codes[:, g, :].bitcast(FP8X4),
-                        lhsT_scale=z_scales[:, g, :],
-                        rhs=w_codes[:, g, n_cols].bitcast(FP8X4),
-                        rhs_scale=w_planes[PACK * g : P, n_cols],
-                        start=(g == 0),
-                        stop=(g == GROUPS - 1),
-                    )
-                out_sb = result.tile([P, N_TILE], F32)
-                nc.scalar.copy(out=out_sb[:], in_=acc[:])
-                nc.sync.dma_start(out=out[i][:, n_cols], in_=out_sb[:])
+        def store(c):
+            if not 0 <= c < TILES * N_TILES:
+                return
+            i, nt = divmod(c, N_TILES)
+            out_sb = result.tile([P, N_TILE], F32, name="out_sb", tag="out_sb")
+            nc.scalar.copy(out=out_sb[:], in_=acc[c][:])
+            nc.sync.dma_start(out=out[i][:, nt * N_TILE : (nt + 1) * N_TILE], in_=out_sb[:])
+
+        head_stats(0)
+        head_stats(1)
+        head_stats(2)
+        nc.vector.tensor_copy(out=chan_affine[:], in_=ln_ps[:, :, 0 : 2 * GROUPS])
+        nc.vector.tensor_copy(out=ghT[:], in_=gh_ps[:])
+        for s in range(UNITS + 9):
+            tile_now, phase = divmod(s, GROUPS)
+            project(s - 7)
+            dot_products(s)
+            ln_affine(s - 3)
+            if phase == 1:
+                norm_scalars(tile_now)
+            dot_sums(s - 1)
+            store(s - 8)
+            head_stats(s + 3)
+            if phase == 0:
+                variance_sums(tile_now)
+            scale_heads(s - 1)
+            if phase == 0:
+                standard_deviation(tile_now)
+            sort_gate_columns(s - 1)
+            to_channels(s - 2)
+            gate_and_round(s - 3)
+            if phase == 2:
+                quantise(tile_now - 1)

@@ -318,7 +318,7 @@ def tile_full_tmix_params_pc_kernel(
                 return
             i, nt = divmod(c, N_TILES)
             out_sb = result.tile([P, N_TILE], F32, name="out_sb", tag="out_sb")
-            nc.scalar.copy(out=out_sb[:], in_=acc[c][:])
+            nc.vector.tensor_copy(out=out_sb[:], in_=acc[c][:])
             nc.sync.dma_start(out=out[i][:, nt * N_TILE : (nt + 1) * N_TILE], in_=out_sb[:])
 
         head_stats(0)

from contextlib import ExitStack

import concourse.mybir as mybir
from concourse.masks import make_identity

F32 = mybir.dt.float32
BF16 = mybir.dt.bfloat16
I32 = mybir.dt.int32
U32 = mybir.dt.uint32
U8 = mybir.dt.uint8
FP8X4 = mybir.dt.float8_e4m3fn_x4
ACT = mybir.ActivationFunctionType
ALU = mybir.AluOpType
AXIS = mybir.AxisListType

P = 128
PACK = 4
K_PASS = P * PACK
TILES = 4
CH = 2048
GROUPS = CH // K_PASS
HEAD = 64
HEADS = CH // HEAD
HEADS_PER_GROUP = K_PASS // HEAD
ROWS_PER_HEAD = HEAD // PACK
HID = 256
HID_HALVES = HID // P
N_TILE = 512
N_TILES = CH // N_TILE
UNITS = TILES * GROUPS
EPS_GN = 0.00064

FLOPS = 2 * TILES * P * CH * CH + 2 * TILES * P * HID * CH


def tile_full_tmix_params_pc_kernel(
    tc, y, r, k, v, g_hid, g2, r_k, ln_g, ln_b, W_o_words, W_o_scales, out
):
    nc = tc.nc
    with ExitStack() as stack:
        stack.enter_context(tc.manual_schedule())
        const = stack.enter_context(tc.tile_pool(name="const", bufs=1))
        inputs = stack.enter_context(tc.tile_pool(name="inputs", bufs=TILES))
        small = stack.enter_context(tc.tile_pool(name="small", bufs=2))
        token = stack.enter_context(tc.tile_pool(name="token", bufs=3))
        chan = stack.enter_context(tc.tile_pool(name="chan", bufs=2))
        quant = stack.enter_context(tc.tile_pool(name="quant", bufs=2))
        result = stack.enter_context(tc.tile_pool(name="result", bufs=3))
        unit_psum = stack.enter_context(tc.psum_pool(name="unit_psum", bufs=2))
        acc_psum = stack.enter_context(tc.psum_pool(name="acc_psum", bufs=2))

        w_planes = const.tile([P, CH], U8, align_bytes=64)
        nc.vector.memset(w_planes[:].bitcast(I32), 0)
        rk_row = const.tile([P, CH], BF16)
        nc.vector.memset(rk_row[:], 0.0)
        ln_rows = const.tile([P, K_PASS], BF16)
        nc.vector.memset(ln_rows[:], 0.0)
        ones = const.tile([P, P], BF16)
        nc.vector.memset(ones[:], 1.0)
        one_col = const.tile([P, 1], F32)
        nc.vector.memset(one_col[:], 1.0)

        y_sb, r_sb, k_sb, v_sb = {}, {}, {}, {}

        def load(dst, src, i, name):
            dst[i] = inputs.tile([P, CH], BF16, name="%s_sb" % name, tag=name)
            nc.sync.dma_start(out=dst[i][:], in_=src[i])

        def load_token_tile(i):
            load(y_sb, y, i, "y")
            load(r_sb, r, i, "r")
            load(k_sb, k, i, "k")
            load(v_sb, v, i, "v")

        w_codes = const.tile([P, GROUPS, CH], U32, align_bytes=64)
        w_words = W_o_words.rearrange("g p n t -> p g (n t)")

        def load_w_columns(nt):
            nc.sync.dma_start(
                out=w_codes[:, :, nt * N_TILE : (nt + 1) * N_TILE].bitcast(I32),
                in_=w_words[:, :, nt * N_TILE * PACK : (nt + 1) * N_TILE * PACK].bitcast(I32),
            )

        nc.sync.dma_start(out=rk_row[0:1, :], in_=r_k.rearrange("h c -> (h c)").unsqueeze(0))
        nc.sync.dma_start(out=ln_rows[0:GROUPS, :], in_=ln_g.rearrange("(g c) -> g c", g=GROUPS))
        nc.sync.dma_start(
            out=ln_rows[GROUPS : 2 * GROUPS, :], in_=ln_b.rearrange("(g c) -> g c", g=GROUPS)
        )
        gh_raw = const.tile([P, TILES, HID], BF16)
        nc.sync.dma_start(out=gh_raw[:], in_=g_hid.rearrange("b t j -> t b j"))
        load_token_tile(0)
        g2_raw = const.tile([P, HID_HALVES, CH], BF16)
        for jh in range(HID_HALVES):
            nc.sync.dma_start(out=g2_raw[:, jh, :], in_=g2[jh * P : (jh + 1) * P, :])
        load_token_tile(1)
        load_token_tile(2)
        for q in range(4):
            nc.sync.dma_start(
                out=w_planes[32 * q : 32 * q + 16, :].bitcast(I32),
                in_=W_o_scales[:, 4 * q : 4 * q + 4, :].bitcast(I32),
            )
        load_w_columns(0)
        load_w_columns(1)
        load(y_sb, y, 3, "y")
        load_w_columns(2)
        load_w_columns(3)
        load(r_sb, r, 3, "r")
        load(k_sb, k, 3, "k")
        load(v_sb, v, 3, "v")

        ident_f32 = const.tile([P, P], F32)
        make_identity(nc, ident_f32[:])
        ident_bf = const.tile([P, P], BF16)
        make_identity(nc, ident_bf[:])

        nc.scalar.activation(out=one_col[:], in_=one_col[:], func=ACT.Sqrt)

        rk_bc = const.tile([P, CH], BF16)
        for nt in range(N_TILES):
            n_cols = slice(nt * N_TILE, (nt + 1) * N_TILE)
            rk_ps = acc_psum.tile([P, N_TILE], F32, tag="acc")
            nc.tensor.matmul(rk_ps[:], lhsT=ones[:], rhs=rk_row[:, n_cols], start=True, stop=True)
            nc.scalar.copy(out=rk_bc[:, n_cols], in_=rk_ps[:])

        ln_sorted = const.tile([P, PACK, P], F32)
        nc.vector.tensor_copy(out=ln_sorted[:], in_=ln_rows[:].rearrange("p (q t) -> p t q", t=PACK))
        ln_ps = unit_psum.tile([P, PACK, P], F32, tag="normT")
        for t in range(PACK):
            nc.tensor.transpose(ln_ps[:, t, :], ln_sorted[:, t, :], ident_f32[:])
        chan_affine = const.tile([P, PACK, 2 * GROUPS], F32)

        gh_ps = unit_psum.tile([P, HID_HALVES, TILES * P], BF16, tag="bonusT")
        for i in range(TILES):
            for jh in range(HID_HALVES):
                nc.tensor.transpose(
                    gh_ps[:, jh, i * P : (i + 1) * P], gh_raw[:, i, jh * P : (jh + 1) * P], ident_bf[:]
                )
        ghT = const.tile([P, HID_HALVES, TILES * P], BF16)
        g2_sorted = const.tile([P, HID_HALVES, GROUPS, PACK, P], BF16)

        stats, m2, mean2, std, rstd, shift = {}, {}, {}, {}, {}, {}
        prod, dot, norm, bonus = {}, {}, {}, {}
        normT, bonusT, gateT, y2T = {}, {}, {}, {}
        zT, z_codes, z_scales, acc = {}, {}, {}, {}

        def head_stats(u):
            if not 0 <= u < UNITS:
                return
            i, g = divmod(u, GROUPS)
            if g == 0:
                stats[i] = small.tile([P, HEADS, 6], F32, name="stats", tag="stats")
            for h in range(g * HEADS_PER_GROUP, (g + 1) * HEADS_PER_GROUP):
                nc.vector.bn_stats(out=stats[i][:, h, :], in_=y_sb[i][:, h * HEAD : (h + 1) * HEAD])

        def variance_sums(i):
            if not 0 <= i < TILES:
                return
            mean_even, m2_even = stats[i][:, :, 1], stats[i][:, :, 2]
            mean_odd, m2_odd = stats[i][:, :, 4], stats[i][:, :, 5]
            diff = small.tile([P, HEADS], F32, name="diff", tag="diff")
            m2[i] = small.tile([P, HEADS], F32, name="m2", tag="m2")
            mean2[i] = small.tile([P, HEADS], F32, name="mean2", tag="mean2")
            nc.vector.tensor_sub(out=diff[:], in0=mean_even, in1=mean_odd)
            nc.vector.scalar_tensor_tensor(
                out=m2[i][:], in0=m2_even, scalar=HEAD * EPS_GN, in1=m2_odd, op0=ALU.add, op1=ALU.add
            )
            nc.vector.tensor_mul(out=diff[:], in0=diff[:], in1=diff[:])
            nc.vector.scalar_tensor_tensor(
                out=m2[i][:], in0=diff[:], scalar=HEAD / 4.0, in1=m2[i][:], op0=ALU.mult, op1=ALU.add
            )
            nc.vector.tensor_add(out=mean2[i][:], in0=mean_even, in1=mean_odd)

        def standard_deviation(i):
            if not 0 <= i < TILES:
                return
            std[i] = small.tile([P, HEADS], F32, name="std", tag="std")
            nc.scalar.activation(out=std[i][:], in_=m2[i][:], func=ACT.Sqrt, scale=1.0 / HEAD)

        def norm_scalars(i):
            if not 0 <= i < TILES:
                return
            rstd[i] = small.tile([P, HEADS], F32, name="rstd", tag="rstd")
            shift[i] = small.tile([P, HEADS], F32, name="shift", tag="shift")
            nc.vector.reciprocal(out=rstd[i][:], in_=std[i][:])
            nc.vector.scalar_tensor_tensor(
                out=shift[i][:], in0=mean2[i][:], scalar=-0.5, in1=rstd[i][:], op0=ALU.mult, op1=ALU.mult
            )

        def dot_products(u):
            if not 0 <= u < UNITS:
                return
            i, g = divmod(u, GROUPS)
            cols = slice(g * K_PASS, (g + 1) * K_PASS)
            prod[u] = token.tile([P, K_PASS], F32, name="prod", tag="prod")
            nc.gpsimd.tensor_tensor(out=prod[u][:], in0=r_sb[i][:, cols], in1=k_sb[i][:, cols], op=ALU.mult)
            nc.gpsimd.tensor_tensor(out=prod[u][:], in0=prod[u][:], in1=rk_bc[:, cols], op=ALU.mult)

        def dot_sums(u):
            if not 0 <= u < UNITS:
                return
            dot[u] = small.tile([P, HEADS_PER_GROUP], F32, name="dot", tag="dot", bufs=4)
            nc.vector.tensor_reduce(
                out=dot[u][:], in_=prod[u][:].rearrange("p (h c) -> p h c", c=HEAD), axis=AXIS.X, op=ALU.add
            )

        def scale_heads(u):
            if not 0 <= u < UNITS:
                return
            i, g = divmod(u, GROUPS)
            norm[u] = token.tile([P, PACK, P], F32, name="norm", tag="norm")
            bonus[u] = token.tile([P, PACK, P], F32, name="bonus", tag="bonus")
            for hh in range(HEADS_PER_GROUP):
                h = g * HEADS_PER_GROUP + hh
                nc.scalar.activation(
                    out=norm[u][:, :, hh * ROWS_PER_HEAD : (hh + 1) * ROWS_PER_HEAD],
                    in_=y_sb[i][:, h * HEAD : (h + 1) * HEAD].rearrange("p (q t) -> p t q", t=PACK),
                    func=ACT.Identity,
                    scale=rstd[i][:, h : h + 1],
                    bias=shift[i][:, h : h + 1],
                )
            for hh in range(HEADS_PER_GROUP):
                h = g * HEADS_PER_GROUP + hh
                nc.scalar.activation(
                    out=bonus[u][:, :, hh * ROWS_PER_HEAD : (hh + 1) * ROWS_PER_HEAD],
                    in_=v_sb[i][:, h * HEAD : (h + 1) * HEAD].rearrange("p (q t) -> p t q", t=PACK),
                    func=ACT.Copy,
                    scale=dot[u][:, hh : hh + 1],
                )

        def sort_gate_columns(g):
            if not 0 <= g < GROUPS:
                return
            for jh in range(HID_HALVES):
                nc.scalar.copy(
                    out=g2_sorted[:, jh, g],
                    in_=g2_raw[:, jh, g * K_PASS : (g + 1) * K_PASS].rearrange("p (q t) -> p t q", t=PACK),
                )

        def to_channels(u):
            if not 0 <= u < UNITS:
                return
            i, g = divmod(u, GROUPS)
            normT[u] = unit_psum.tile([P, PACK, P], F32, name="normT", tag="normT")
            for t in range(PACK):
                nc.tensor.transpose(normT[u][:, t, :], norm[u][:, t, :], ident_f32[:])
            bonusT[u] = unit_psum.tile([P, PACK, P], F32, name="bonusT", tag="bonusT")
            for t in range(PACK):
                nc.tensor.transpose(bonusT[u][:, t, :], bonus[u][:, t, :], ident_f32[:])
            gateT[u] = unit_psum.tile([P, PACK, P], F32, name="gateT", tag="gateT")
            for t in range(PACK):
                for jh in range(HID_HALVES):
                    nc.tensor.matmul(
                        gateT[u][:, t, :],
                        lhsT=g2_sorted[:, jh, g, t, :],
                        rhs=ghT[:, jh, i * P : (i + 1) * P],
                        start=(jh == 0),
                        stop=(jh == HID_HALVES - 1),
                    )

        def ln_affine(u):
            if not 0 <= u < UNITS:
                return
            g = u % GROUPS
            y2T[u] = chan.tile([P, PACK, P], F32, name="y2T", tag="y2T")
            for t in range(PACK):
                nc.scalar.activation(
                    out=y2T[u][:, t, :],
                    in_=normT[u][:, t, :],
                    func=ACT.Identity,
                    scale=chan_affine[:, t, g : g + 1],
                    bias=chan_affine[:, t, GROUPS + g : GROUPS + g + 1],
                )

        def gate_and_round(u):
            if not 0 <= u < UNITS:
                return
            i, g = divmod(u, GROUPS)
            if g == 0:
                zT[i] = quant.tile([P, GROUPS, P, PACK], BF16, name="zT", tag="zT", align_bytes=64)
            nc.vector.tensor_tensor(out=y2T[u][:], in0=y2T[u][:], in1=bonusT[u][:], op=ALU.add)
            nc.vector.tensor_tensor(
                out=zT[i][:, g],
                in0=y2T[u][:].rearrange("p t m -> p m t"),
                in1=gateT[u][:].rearrange("p t m -> p m t"),
                op=ALU.mult,
            )

        def quantise(i):
            if not 0 <= i < TILES:
                return
            z_codes[i] = quant.tile([P, GROUPS, P], U32, name="z_codes", tag="z_codes", align_bytes=64)
            z_scales[i] = quant.tile([P, GROUPS, P], U8, name="z_scales", tag="z_scales", align_bytes=64)
            nc.vector.quantize_mx(
                out=z_codes[i][:].rearrange("p g m -> p (g m)").bitcast(FP8X4),
                scales=z_scales[i][:].rearrange("p g m -> p (g m)"),
                in_=zT[i][:].rearrange("p g m t -> p (g m t)"),
            )

        def project(c):
            if not 0 <= c < TILES * N_TILES:
                return
            i, nt = divmod(c, N_TILES)
            n_cols = slice(nt * N_TILE, (nt + 1) * N_TILE)
            acc[c] = acc_psum.tile([P, N_TILE], F32, name="acc", tag="acc")
            for g in range(GROUPS):
                nc.tensor.matmul_mx(
                    out=acc[c][:],
                    lhsT=z_codes[i][:, g, :].bitcast(FP8X4),
                    lhsT_scale=z_scales[i][:, g, :],
                    rhs=w_codes[:, g, n_cols].bitcast(FP8X4),
                    rhs_scale=w_planes[PACK * g : P, n_cols],
                    start=(g == 0),
                    stop=(g == GROUPS - 1),
                )

        def store(c):
            if not 0 <= c < TILES * N_TILES:
                return
            i, nt = divmod(c, N_TILES)
            out_sb = result.tile([P, N_TILE], F32, name="out_sb", tag="out_sb")
            nc.vector.tensor_copy(out=out_sb[:], in_=acc[c][:])
            nc.sync.dma_start(out=out[i][:, nt * N_TILE : (nt + 1) * N_TILE], in_=out_sb[:])

        head_stats(0)
        head_stats(1)
        head_stats(2)
        nc.vector.tensor_copy(out=chan_affine[:], in_=ln_ps[:, :, 0 : 2 * GROUPS])
        nc.vector.tensor_copy(out=ghT[:], in_=gh_ps[:])
        for s in range(UNITS + 9):
            tile_now, phase = divmod(s, GROUPS)
            project(s - 7)
            dot_products(s)
            ln_affine(s - 3)
            if phase == 1:
                norm_scalars(tile_now)
            dot_sums(s - 1)
            store(s - 8)
            head_stats(s + 3)
            if phase == 0:
                variance_sums(tile_now)
            scale_heads(s - 1)
            if phase == 0:
                standard_deviation(tile_now)
            sort_gate_columns(s - 1)
            to_channels(s - 2)
            gate_and_round(s - 3)
            if phase == 2:
                quantise(tile_now - 1)
